import numpy as np
import ml_dtypes


def mxq(x, axis, fmt="e4m3"):
    dtype, down = {"e4m3": (ml_dtypes.float8_e4m3fn, 7), "e5m2": (ml_dtypes.float8_e5m2, 14)}[fmt]
    v = np.moveaxis(np.asarray(x, np.float32).astype(ml_dtypes.bfloat16).astype(np.float64), axis, -1)
    blocks = v.reshape(v.shape[:-1] + (-1, 32))
    amax = np.abs(blocks).max(-1, keepdims=True)
    byte = np.maximum(np.where(amax > 0, np.frexp(amax)[1] - 1 + 127, 0) - down, 1)
    scale = np.exp2(byte - 127.0)
    codes = (blocks / scale).astype(np.float32).astype(dtype).astype(np.float64)
    return np.moveaxis((codes * scale).reshape(v.shape), -1, axis)


WIDE = False


def mx_kscale(k):
    if not WIDE:
        return np.ones(k)
    levels = np.array([10, -10, 5, -5, 0])
    a = np.random.permutation(np.resize(levels, k // 512 * 4)).reshape(k // 512, 4)
    idx = np.arange(k)
    return np.exp2(a[idx // 512, idx % 128 // 32])


BF16 = ml_dtypes.bfloat16


def bf(x):
    return np.asarray(x, np.float32).astype(BF16)


def f64(x):
    return np.asarray(x).astype(np.float64)


B, C, O, ROWS, COLS, KH, KW = 64, 64, 128, 8, 8, 4, 4
H, W, K = ROWS + KH - 1, COLS + KW - 1, C * KH * KW


def setup_inputs():
    sc = mx_kscale(K)[::KH * KW]
    return {"x": bf(np.random.standard_normal((B, C, H, W)) * sc[None, :, None, None]),
            "weight": bf(np.random.standard_normal((ROWS, COLS, O, C, KH, KW)) / np.sqrt(K) / sc[None, None, None, :, None, None])}


def reference(x, weight):
    x, weight = f64(x), f64(weight)
    rows, cols, o, c, kh, kw = weight.shape
    b = x.shape[0]
    patches = np.stack(
        [np.stack([x[:, :, u:u + rows, v:v + cols] for v in range(kw)], axis=2)
         for u in range(kh)], axis=2)
    p = patches.transpose(4, 5, 0, 1, 2, 3).reshape(rows * cols, b, c * kh * kw)
    w = weight.reshape(rows * cols, o, c * kh * kw)
    y = mxq(p, 2, "e4m3") @ mxq(w, 2, "e4m3").transpose(0, 2, 1)
    return y.reshape(rows, cols, b, o).transpose(2, 3, 0, 1)

@@ -1,0 +1,160 @@
+from contextlib import ExitStack
+
+import concourse.mybir as mybir
+from concourse.masks import make_identity
+
+F32 = mybir.dt.float32
+BF16 = mybir.dt.bfloat16
+U32 = mybir.dt.uint32
+U8 = mybir.dt.uint8
+FP8X4 = mybir.dt.float8_e4m3fn_x4
+
+P = 128
+B, C, O, ROWS, COLS, KH, KW = 64, 64, 128, 8, 8, 4, 4
+HW = 121
+K = C * KH * KW
+NPOS = ROWS * COLS
+GRP = 4
+NG = NPOS // GRP
+XROW = 96
+XLEN = 88
+WBUFS = 5
+ROW_START = 4
+FLOPS = 2 * NPOS * B * O * K
+
+
+def tile_localconvolution_kernel(tc, x, weight, out):
+    nc = tc.nc
+    w_view = weight.rearrange("i j o c u v -> o (i j) (c u v)")
+    x_view = x.rearrange("b c h w -> c b (h w)")
+    out_view = out.rearrange("b o i j -> o b (i j)")
+
+    with ExitStack() as ctx:
+        keep = ctx.enter_context(tc.tile_pool(name="keep", bufs=1))
+        wraw_pool = ctx.enter_context(tc.tile_pool(name="wraw", bufs=WBUFS))
+        gw_pool = ctx.enter_context(tc.tile_pool(name="gw", bufs=3))
+        wq_pool = ctx.enter_context(tc.tile_pool(name="wq", bufs=8))
+        gp_pool = ctx.enter_context(tc.tile_pool(name="gp", bufs=2))
+        wt_pool = ctx.enter_context(tc.psum_pool(name="wt", bufs=6))
+        acc_pool = ctx.enter_context(tc.psum_pool(name="acc", bufs=2))
+        ctx.enter_context(tc.manual_schedule())
+
+        ident = keep.tile([P, P], F32, name="ident")
+        make_identity(nc, ident[:])
+        xt = keep.tile([P, 2, B, XROW], BF16, name="xt")
+        pc = keep.tile([P, ROWS, 2, COLS * B], U32, name="pc", align_bytes=64)
+        ps = keep.tile([P, ROWS, 2, COLS * B], U8, name="ps", align_bytes=64)
+        res = keep.tile([P, B, NPOS], F32, name="res")
+
+        wraw = {}
+        gw = {}
+        wc = {}
+        ws = {}
+
+        def load_w(n):
+            t = wraw_pool.tile([P, GRP, K], BF16, name="wraw")
+            nc.sync.dma_start(out=t[:], in_=w_view[:, GRP * n:GRP * (n + 1), :])
+            wraw[n] = t
+
+        def load_x(u, g):
+            nc.sync.dma_start(
+                out=xt[u:P:KH, g, :, 0:XLEN],
+                in_=x_view[32 * g:32 * (g + 1), :, 11 * u:11 * u + XLEN],
+            )
+
+        def transpose_group(n):
+            wf = wraw[n][:].bitcast(F32)
+            g_t = gw_pool.tile([P, GRP, 2, O, 4], BF16, name="gw", align_bytes=64)
+            gw[n] = g_t
+            gf = g_t[:].bitcast(F32)
+            for a in range(GRP):
+                bank = wt_pool.tile([P, 512], F32, name="wt")
+                for g in range(2):
+                    for vh in range(2):
+                        s = 2 * g + vh
+                        nc.tensor.transpose(
+                            bank[:, P * s:P * (s + 1)],
+                            wf[:, a, 256 * g + vh:256 * (g + 1):2],
+                            ident[:],
+                        )
+                nc.scalar.copy(
+                    out=gf[:, a],
+                    in_=bank[:].rearrange("p (g v o) -> p g o v", g=2, v=2),
+                )
+
+        def quantise_group(n):
+            c_t = wq_pool.tile([P, GRP * 2 * O], U32, name="wc", align_bytes=64)
+            s_t = wq_pool.tile([P, GRP * 2 * O], U8, name="ws", align_bytes=64)
+            wc[n] = c_t
+            ws[n] = s_t
+            nc.vector.quantize_mx(
+                out=c_t[:].bitcast(FP8X4),
+                scales=s_t[:],
+                in_=gw[n][:].rearrange("p a g o t -> p (a g o t)"),
+            )
+
+        def patch_row(i):
+            gp = gp_pool.tile([P, 2, COLS, B, KW], BF16, name="gp", align_bytes=64)
+            for jr in range(4):
+                nc.vector.tensor_copy(
+                    out=gp[:, :, jr:COLS:4, :, :],
+                    in_=xt[:, :, :, 11 * i + jr:11 * i + jr + 8].rearrange(
+                        "p g b (q v) -> p g q b v", q=2),
+                )
+            nc.vector.quantize_mx(
+                out=pc[:, i].rearrange("p g n -> p (g n)").bitcast(FP8X4),
+                scales=ps[:, i].rearrange("p g n -> p (g n)"),
+                in_=gp[:].rearrange("p g j b v -> p (g j b v)"),
+            )
+
+        def multiply_group(n):
+            i, jh = n // 2, n % 2
+            acc = acc_pool.tile([P, 512], F32, name="acc")
+            for a in range(GRP):
+                q = 2 * jh + a // 2
+                for g in range(2):
+                    lo = (2 * a + g) * O
+                    nc.tensor.matmul_mx(
+                        out=acc[:, P * a:P * (a + 1)],
+                        lhsT=wc[n][:, lo:lo + O].bitcast(FP8X4),
+                        lhsT_scale=ws[n][:, lo:lo + O],
+                        rhs=pc[:, i, g, P * q:P * (q + 1)].bitcast(FP8X4),
+                        rhs_scale=ps[:, i, g, P * q:P * (q + 1)],
+                        start=(g == 0),
+                        stop=(g == 1),
+                    )
+            first = COLS * i + GRP * jh
+            nc.scalar.copy(
+                out=res[:, :, first:first + GRP].rearrange("p b (q r) -> p b q r", q=2),
+                in_=acc[:].rearrange("p (q c b) -> p q c b", q=2, c=4)[:, :, 0:4:3, :]
+                .rearrange("p q r b -> p b q r"),
+            )
+
+        load_w(0)
+        xs = [(u, g) for g in range(2) for u in range(KH)]
+        for n in range(1, WBUFS):
+            for u, g in xs[2 * (n - 1):2 * n]:
+                load_x(u, g)
+            load_w(n)
+
+        next_m = 0
+        row_done = {}
+        for n in range(NG + 2):
+            if n < NG:
+                transpose_group(n)
+                if n + WBUFS < NG:
+                    load_w(n + WBUFS)
+            if 1 <= n <= NG:
+                quantise_group(n - 1)
+            i = n - ROW_START
+            if 0 <= i < ROWS:
+                patch_row(i)
+                row_done[i] = n
+            count = 0
+            while (next_m < NG and next_m <= n - 2 and count < 2
+                   and row_done.get(next_m // 2, n) < n):
+                multiply_group(next_m)
+                next_m += 1
+                count += 1
+
+        nc.sync.dma_start(out=out_view, in_=res[:])

@@ -11,56 +11,72 @@ FP8X4 = mybir.dt.float8_e4m3fn_x4
 
 P = 128
 B, C, O, ROWS, COLS, KH, KW = 64, 64, 128, 8, 8, 4, 4
-HW = 121
+H = 11
+XLEN = C * H * H
 K = C * KH * KW
 NPOS = ROWS * COLS
 GRP = 4
 NG = NPOS // GRP
-XROW = 96
-XLEN = 88
 WBUFS = 5
-ROW_START = 4
+ROW_SEQ = [0, 4, 1, 5, 2, 6, 3, 7]
+SUBS_PER_STEP = [1, 2, 1] * 4
 FLOPS = 2 * NPOS * B * O * K
 
 
 def tile_localconvolution_kernel(tc, x, weight, out):
     nc = tc.nc
     w_view = weight.rearrange("i j o c u v -> o (i j) (c u v)")
-    x_view = x.rearrange("b c h w -> c b (h w)")
+    x_flat = x.rearrange("b c h w -> b (c h w)")
     out_view = out.rearrange("b o i j -> o b (i j)")
 
     with ExitStack() as ctx:
         keep = ctx.enter_context(tc.tile_pool(name="keep", bufs=1))
         wraw_pool = ctx.enter_context(tc.tile_pool(name="wraw", bufs=WBUFS))
         gw_pool = ctx.enter_context(tc.tile_pool(name="gw", bufs=3))
-        wq_pool = ctx.enter_context(tc.tile_pool(name="wq", bufs=8))
+        wq_pool = ctx.enter_context(tc.tile_pool(name="wq", bufs=6))
+        pi_pool = ctx.enter_context(tc.tile_pool(name="pi", bufs=3))
         gp_pool = ctx.enter_context(tc.tile_pool(name="gp", bufs=2))
-        wt_pool = ctx.enter_context(tc.psum_pool(name="wt", bufs=6))
+        tp_pool = ctx.enter_context(tc.psum_pool(name="tp", bufs=6))
         acc_pool = ctx.enter_context(tc.psum_pool(name="acc", bufs=2))
         ctx.enter_context(tc.manual_schedule())
 
         ident = keep.tile([P, P], F32, name="ident")
         make_identity(nc, ident[:])
-        xt = keep.tile([P, 2, B, XROW], BF16, name="xt")
-        pc = keep.tile([P, ROWS, 2, COLS * B], U32, name="pc", align_bytes=64)
-        ps = keep.tile([P, ROWS, 2, COLS * B], U8, name="ps", align_bytes=64)
+        xs = keep.tile([P, XLEN], BF16, name="xs")
+        pc = keep.tile([P, 4, COLS, 2, P], U32, name="pc", align_bytes=64)
+        ps = keep.tile([P, 4, COLS, 2, P], U8, name="ps", align_bytes=64)
         res = keep.tile([P, B, NPOS], F32, name="res")
 
         wraw = {}
         gw = {}
         wc = {}
         ws = {}
+        pim = {}
+        gp = {}
+
+        def group_pos(n):
+            return ROW_SEQ[n // 2], n % 2
 
         def load_w(n):
+            i, jh = group_pos(n)
+            first = COLS * i + GRP * jh
             t = wraw_pool.tile([P, GRP, K], BF16, name="wraw")
-            nc.sync.dma_start(out=t[:], in_=w_view[:, GRP * n:GRP * (n + 1), :])
+            nc.sync.dma_start(out=t[:], in_=w_view[:, first:first + GRP, :])
             wraw[n] = t
 
-        def load_x(u, g):
-            nc.sync.dma_start(
-                out=xt[u:P:KH, g, :, 0:XLEN],
-                in_=x_view[32 * g:32 * (g + 1), :, 11 * u:11 * u + XLEN],
-            )
+        def flip(src_words, dst_words, engine):
+            bank = tp_pool.tile([P, 512], F32, name="tp")
+            for ch in range(4):
+                nc.tensor.transpose(
+                    bank[:, P * ch:P * (ch + 1)],
+                    src_words[:, P * ch:P * (ch + 1)],
+                    ident[:],
+                )
+            view = bank[:].rearrange("p (g m n) -> p g n m", g=2, m=2)
+            if engine == "s":
+                nc.scalar.copy(out=dst_words, in_=view)
+            else:
+                nc.vector.tensor_copy(out=dst_words, in_=view)
 
         def transpose_group(n):
             wf = wraw[n][:].bitcast(F32)
@@ -68,19 +84,7 @@ def tile_localconvolution_kernel(tc, x, weight, out):
             gw[n] = g_t
             gf = g_t[:].bitcast(F32)
             for a in range(GRP):
-                bank = wt_pool.tile([P, 512], F32, name="wt")
-                for g in range(2):
-                    for vh in range(2):
-                        s = 2 * g + vh
-                        nc.tensor.transpose(
-                            bank[:, P * s:P * (s + 1)],
-                            wf[:, a, 256 * g + vh:256 * (g + 1):2],
-                            ident[:],
-                        )
-                nc.scalar.copy(
-                    out=gf[:, a],
-                    in_=bank[:].rearrange("p (g v o) -> p g o v", g=2, v=2),
-                )
+                flip(wf[:, a], gf[:, a], "s")
 
         def quantise_group(n):
             c_t = wq_pool.tile([P, GRP * 2 * O], U32, name="wc", align_bytes=64)
@@ -93,66 +97,95 @@ def tile_localconvolution_kernel(tc, x, weight, out):
                 in_=gw[n][:].rearrange("p a g o t -> p (a g o t)"),
             )
 
-        def patch_row(i):
-            gp = gp_pool.tile([P, 2, COLS, B, KW], BF16, name="gp", align_bytes=64)
-            for jr in range(4):
-                nc.vector.tensor_copy(
-                    out=gp[:, :, jr:COLS:4, :, :],
-                    in_=xt[:, :, :, 11 * i + jr:11 * i + jr + 8].rearrange(
-                        "p g b (q v) -> p g q b v", q=2),
-                )
+        def im2col(sub):
+            r, jr = sub // 4, sub % 4
+            t = pi_pool.tile([P, 2, K], BF16, name="pim")
+            pim[sub] = t
+            nc.vector.tensor_copy(
+                out=t[:].rearrange("p q (c u v) -> p q c u v", c=C, u=KH),
+                in_=xs[:].rearrange("p (c h w) -> p c h w", c=C, h=H)[
+                    :, :, r:r + KH, jr:jr + 2 * KW].rearrange(
+                    "p c u (q v) -> p q c u v", q=2),
+            )
+
+        def transpose_sub(sub):
+            half = sub // 2
+            if sub % 2 == 0:
+                gp[half] = gp_pool.tile([P, 4, 2, P, 4], BF16, name="gp", align_bytes=64)
+            gf = gp[half][:].bitcast(F32)
+            pf = pim[sub][:].bitcast(F32)
+            for q in range(2):
+                flip(pf[:, q], gf[:, 2 * (sub % 2) + q], "s" if q == 0 else "v")
+
+        def quantise_half(half):
+            r, hh = half // 2, half % 2
             nc.vector.quantize_mx(
-                out=pc[:, i].rearrange("p g n -> p (g n)").bitcast(FP8X4),
-                scales=ps[:, i].rearrange("p g n -> p (g n)"),
-                in_=gp[:].rearrange("p g j b v -> p (g j b v)"),
+                out=pc[:, r, 4 * hh:4 * hh + 4].rearrange("p a g n -> p (a g n)").bitcast(FP8X4),
+                scales=ps[:, r, 4 * hh:4 * hh + 4].rearrange("p a g n -> p (a g n)"),
+                in_=gp[half][:].rearrange("p a g n t -> p (a g n t)"),
             )
 
         def multiply_group(n):
-            i, jh = n // 2, n % 2
+            i, jh = group_pos(n)
+            r, s = i % 4, i // 4
             acc = acc_pool.tile([P, 512], F32, name="acc")
             for a in range(GRP):
-                q = 2 * jh + a // 2
                 for g in range(2):
                     lo = (2 * a + g) * O
                     nc.tensor.matmul_mx(
                         out=acc[:, P * a:P * (a + 1)],
                         lhsT=wc[n][:, lo:lo + O].bitcast(FP8X4),
                         lhsT_scale=ws[n][:, lo:lo + O],
-                        rhs=pc[:, i, g, P * q:P * (q + 1)].bitcast(FP8X4),
-                        rhs_scale=ps[:, i, g, P * q:P * (q + 1)],
+                        rhs=pc[:, r, 2 * a + jh, g, :].bitcast(FP8X4),
+                        rhs_scale=ps[:, r, 2 * a + jh, g, :],
                         start=(g == 0),
                         stop=(g == 1),
                     )
             first = COLS * i + GRP * jh
             nc.scalar.copy(
-                out=res[:, :, first:first + GRP].rearrange("p b (q r) -> p b q r", q=2),
-                in_=acc[:].rearrange("p (q c b) -> p q c b", q=2, c=4)[:, :, 0:4:3, :]
-                .rearrange("p q r b -> p b q r"),
+                out=res[:, :, first:first + GRP],
+                in_=acc[:].rearrange("p (a b s) -> p s b a", a=GRP, s=2)[:, s],
             )
 
+        subs_at = {}
+        nxt = 0
+        for t, cnt in enumerate(SUBS_PER_STEP):
+            subs_at[t] = list(range(nxt, nxt + cnt))
+            nxt += cnt
+
         load_w(0)
-        xs = [(u, g) for g in range(2) for u in range(KH)]
+        nc.sync.dma_start(out=xs[0:P:2, :], in_=x_flat)
+        nc.sync.dma_start(out=xs[1:P:2, 0:XLEN - 4 * H], in_=x_flat[:, 4 * H:XLEN])
         for n in range(1, WBUFS):
-            for u, g in xs[2 * (n - 1):2 * n]:
-                load_x(u, g)
             load_w(n)
+        for sub in subs_at[0]:
+            im2col(sub)
 
         next_m = 0
-        row_done = {}
-        for n in range(NG + 2):
-            if n < NG:
-                transpose_group(n)
-                if n + WBUFS < NG:
-                    load_w(n + WBUFS)
-            if 1 <= n <= NG:
-                quantise_group(n - 1)
-            i = n - ROW_START
-            if 0 <= i < ROWS:
-                patch_row(i)
-                row_done[i] = n
+        half_step = {}
+        pending_half = []
+        for t in range(NG + 2):
+            if 1 <= t <= NG:
+                quantise_group(t - 1)
+            for half in pending_half:
+                quantise_half(half)
+                half_step[half] = t
+            pending_half = []
+            for sub in subs_at.get(t + 1, []):
+                im2col(sub)
+            if t < NG:
+                transpose_group(t)
+                if t + WBUFS < NG:
+                    load_w(t + WBUFS)
+            for sub in subs_at.get(t, []):
+                transpose_sub(sub)
+                if sub % 2 == 1:
+                    pending_half.append(sub // 2)
             count = 0
-            while (next_m < NG and next_m <= n - 2 and count < 2
-                   and row_done.get(next_m // 2, n) < n):
+            while next_m < NG and next_m <= t - 2 and count < 2:
+                r = group_pos(next_m)[0] % 4
+                if half_step.get(2 * r + 1, t) >= t:
+                    break
                 multiply_group(next_m)
                 next_m += 1
                 count += 1

@@ -17,9 +17,12 @@ K = C * KH * KW
 NPOS = ROWS * COLS
 GRP = 4
 NG = NPOS // GRP
+NSUB = 16
 WBUFS = 5
-ROW_SEQ = [0, 4, 1, 5, 2, 6, 3, 7]
-SUBS_PER_STEP = [1, 2, 1] * 4
+LEAD = 1
+HEAD_SUBS = 3
+XQ = 4
+EARLY_GROUPS = 12
 FLOPS = 2 * NPOS * B * O * K
 
 
@@ -34,7 +37,7 @@ def tile_localconvolution_kernel(tc, x, weight, out):
         wraw_pool = ctx.enter_context(tc.tile_pool(name="wraw", bufs=WBUFS))
         gw_pool = ctx.enter_context(tc.tile_pool(name="gw", bufs=3))
         wq_pool = ctx.enter_context(tc.tile_pool(name="wq", bufs=6))
-        pi_pool = ctx.enter_context(tc.tile_pool(name="pi", bufs=3))
+        pi_pool = ctx.enter_context(tc.tile_pool(name="pi", bufs=HEAD_SUBS))
         gp_pool = ctx.enter_context(tc.tile_pool(name="gp", bufs=2))
         tp_pool = ctx.enter_context(tc.psum_pool(name="tp", bufs=6))
         acc_pool = ctx.enter_context(tc.psum_pool(name="acc", bufs=2))
@@ -46,6 +49,7 @@ def tile_localconvolution_kernel(tc, x, weight, out):
         pc = keep.tile([P, 4, COLS, 2, P], U32, name="pc", align_bytes=64)
         ps = keep.tile([P, 4, COLS, 2, P], U8, name="ps", align_bytes=64)
         res = keep.tile([P, B, NPOS], F32, name="res")
+        xs_img = xs[:].rearrange("p (c h w) -> p c h w", c=C, h=H)
 
         wraw = {}
         gw = {}
@@ -54,15 +58,16 @@ def tile_localconvolution_kernel(tc, x, weight, out):
         pim = {}
         gp = {}
 
-        def group_pos(n):
-            return ROW_SEQ[n // 2], n % 2
-
         def load_w(n):
-            i, jh = group_pos(n)
-            first = COLS * i + GRP * jh
             t = wraw_pool.tile([P, GRP, K], BF16, name="wraw")
-            nc.sync.dma_start(out=t[:], in_=w_view[:, first:first + GRP, :])
+            nc.sync.dma_start(out=t[:], in_=w_view[:, GRP * n:GRP * (n + 1), :])
             wraw[n] = t
+
+        def load_x(cq):
+            lo, hi = XLEN // XQ * cq, XLEN // XQ * (cq + 1)
+            nc.sync.dma_start(out=xs[0:P:2, lo:hi], in_=x_flat[:, lo:hi])
+            hi = min(hi, XLEN - H)
+            nc.sync.dma_start(out=xs[1:P:2, lo:hi], in_=x_flat[:, lo + H:hi + H])
 
         def flip(src_words, dst_words, engine):
             bank = tp_pool.tile([P, 512], F32, name="tp")
@@ -97,15 +102,14 @@ def tile_localconvolution_kernel(tc, x, weight, out):
                 in_=gw[n][:].rearrange("p a g o t -> p (a g o t)"),
             )
 
-        def im2col(sub):
+        def im2col(sub, c0, c1):
             r, jr = sub // 4, sub % 4
-            t = pi_pool.tile([P, 2, K], BF16, name="pim")
-            pim[sub] = t
+            if c0 == 0:
+                pim[sub] = pi_pool.tile([P, 2, K], BF16, name="pim")
             nc.vector.tensor_copy(
-                out=t[:].rearrange("p q (c u v) -> p q c u v", c=C, u=KH),
-                in_=xs[:].rearrange("p (c h w) -> p c h w", c=C, h=H)[
-                    :, :, r:r + KH, jr:jr + 2 * KW].rearrange(
-                    "p c u (q v) -> p q c u v", q=2),
+                out=pim[sub][:].rearrange("p q (c u v) -> p c u q v", c=C, u=KH)[:, c0:c1],
+                in_=xs_img[:, c0:c1, 2 * r:2 * r + KH, jr:jr + 2 * KW].rearrange(
+                    "p c u (q v) -> p c u q v", q=2),
             )
 
         def transpose_sub(sub):
@@ -126,8 +130,8 @@ def tile_localconvolution_kernel(tc, x, weight, out):
             )
 
         def multiply_group(n):
-            i, jh = group_pos(n)
-            r, s = i % 4, i // 4
+            i, jh = n // 2, n % 2
+            r, s = i // 2, i % 2
             acc = acc_pool.tile([P, 512], F32, name="acc")
             for a in range(GRP):
                 for g in range(2):
@@ -141,53 +145,51 @@ def tile_localconvolution_kernel(tc, x, weight, out):
                         start=(g == 0),
                         stop=(g == 1),
                     )
-            first = COLS * i + GRP * jh
             nc.scalar.copy(
-                out=res[:, :, first:first + GRP],
+                out=res[:, :, GRP * n:GRP * (n + 1)],
                 in_=acc[:].rearrange("p (a b s) -> p s b a", a=GRP, s=2)[:, s],
             )
 
-        subs_at = {}
-        nxt = 0
-        for t, cnt in enumerate(SUBS_PER_STEP):
-            subs_at[t] = list(range(nxt, nxt + cnt))
-            nxt += cnt
-
-        load_w(0)
-        nc.sync.dma_start(out=xs[0:P:2, :], in_=x_flat)
-        nc.sync.dma_start(out=xs[1:P:2, 0:XLEN - 4 * H], in_=x_flat[:, 4 * H:XLEN])
-        for n in range(1, WBUFS):
+        for cq in range(XQ):
+            load_x(cq)
+        for n in range(WBUFS):
             load_w(n)
-        for sub in subs_at[0]:
-            im2col(sub)
+        cw = C // XQ
+        for cq in range(XQ):
+            for sub in range(HEAD_SUBS):
+                im2col(sub, cw * cq, cw * (cq + 1))
 
         next_m = 0
         half_step = {}
         pending_half = []
-        for t in range(NG + 2):
-            if 1 <= t <= NG:
-                quantise_group(t - 1)
+        for t in range(NG + LEAD + 3):
+            w = t - LEAD
+            if 1 <= w <= NG:
+                quantise_group(w - 1)
             for half in pending_half:
                 quantise_half(half)
                 half_step[half] = t
             pending_half = []
-            for sub in subs_at.get(t + 1, []):
-                im2col(sub)
-            if t < NG:
-                transpose_group(t)
-                if t + WBUFS < NG:
-                    load_w(t + WBUFS)
-            for sub in subs_at.get(t, []):
-                transpose_sub(sub)
-                if sub % 2 == 1:
-                    pending_half.append(sub // 2)
+            if HEAD_SUBS <= t + 1 < NSUB:
+                im2col(t + 1, 0, C)
+            if 0 <= w < NG:
+                transpose_group(w)
+                if w + WBUFS < NG:
+                    load_w(w + WBUFS)
+            if t < NSUB:
+                transpose_sub(t)
+                if t % 2 == 1:
+                    pending_half.append(t // 2)
             count = 0
-            while next_m < NG and next_m <= t - 2 and count < 2:
-                r = group_pos(next_m)[0] % 4
-                if half_step.get(2 * r + 1, t) >= t:
+            while next_m < NG and next_m <= w - 2 and count < 2:
+                if half_step.get(2 * (next_m // 4) + 1, t) >= t:
                     break
                 multiply_group(next_m)
                 next_m += 1
                 count += 1
+                if next_m == EARLY_GROUPS:
+                    done = GRP * EARLY_GROUPS
+                    nc.sync.dma_start(out=out_view[:, :, 0:done], in_=res[:, :, 0:done])
 
-        nc.sync.dma_start(out=out_view, in_=res[:])
+        done = GRP * EARLY_GROUPS
+        nc.sync.dma_start(out=out_view[:, :, done:NPOS], in_=res[:, :, done:NPOS])

@@ -88,8 +88,7 @@ def tile_localconvolution_kernel(tc, x, weight, out):
             g_t = gw_pool.tile([P, GRP, 2, O, 4], BF16, name="gw", align_bytes=64)
             gw[n] = g_t
             gf = g_t[:].bitcast(F32)
-            for a in range(GRP):
-                flip(wf[:, a], gf[:, a], "s")
+            return [(wf[:, a], gf[:, a], "s") for a in range(GRP)]
 
         def quantise_group(n):
             c_t = wq_pool.tile([P, GRP * 2 * O], U32, name="wc", align_bytes=64)
@@ -118,8 +117,7 @@ def tile_localconvolution_kernel(tc, x, weight, out):
                 gp[half] = gp_pool.tile([P, 4, 2, P, 4], BF16, name="gp", align_bytes=64)
             gf = gp[half][:].bitcast(F32)
             pf = pim[sub][:].bitcast(F32)
-            for q in range(2):
-                flip(pf[:, q], gf[:, 2 * (sub % 2) + q], "s" if q == 0 else "v")
+            return [(pf[:, q], gf[:, 2 * (sub % 2) + q], "s" if q == 0 else "v") for q in range(2)]
 
         def quantise_half(half):
             r, hh = half // 2, half % 2
@@ -129,11 +127,15 @@ def tile_localconvolution_kernel(tc, x, weight, out):
                 in_=gp[half][:].rearrange("p a g n t -> p (a g n t)"),
             )
 
-        def multiply_group(n):
+        accs = {}
+
+        def multiply_half(n, part):
             i, jh = n // 2, n % 2
             r, s = i // 2, i % 2
-            acc = acc_pool.tile([P, 512], F32, name="acc")
-            for a in range(GRP):
+            if part == 0:
+                accs[n] = acc_pool.tile([P, 512], F32, name="acc")
+            acc = accs[n]
+            for a in range(2 * part, 2 * part + 2):
                 for g in range(2):
                     lo = (2 * a + g) * O
                     nc.tensor.matmul_mx(
@@ -145,10 +147,11 @@ def tile_localconvolution_kernel(tc, x, weight, out):
                         start=(g == 0),
                         stop=(g == 1),
                     )
-            nc.scalar.copy(
-                out=res[:, :, GRP * n:GRP * (n + 1)],
-                in_=acc[:].rearrange("p (a b s) -> p s b a", a=GRP, s=2)[:, s],
-            )
+            if part == 1:
+                nc.scalar.copy(
+                    out=res[:, :, GRP * n:GRP * (n + 1)],
+                    in_=acc[:].rearrange("p (a b s) -> p s b a", a=GRP, s=2)[:, s],
+                )
 
         for cq in range(XQ):
             load_x(cq)
@@ -172,24 +175,31 @@ def tile_localconvolution_kernel(tc, x, weight, out):
             pending_half = []
             if HEAD_SUBS <= t + 1 < NSUB:
                 im2col(t + 1, 0, C)
+            flips = []
             if 0 <= w < NG:
-                transpose_group(w)
-                if w + WBUFS < NG:
-                    load_w(w + WBUFS)
+                flips.extend(transpose_group(w))
             if t < NSUB:
-                transpose_sub(t)
+                flips.extend(transpose_sub(t))
                 if t % 2 == 1:
                     pending_half.append(t // 2)
-            count = 0
-            while next_m < NG and next_m <= w - 2 and count < 2:
+            halves = []
+            while next_m < NG and next_m <= w - 2 and len(halves) < 4:
                 if half_step.get(2 * (next_m // 4) + 1, t) >= t:
                     break
-                multiply_group(next_m)
+                halves.extend([(next_m, 0), (next_m, 1)])
                 next_m += 1
-                count += 1
-                if next_m == EARLY_GROUPS:
-                    done = GRP * EARLY_GROUPS
-                    nc.sync.dma_start(out=out_view[:, :, 0:done], in_=res[:, :, 0:done])
+            cut_f = (len(flips) + 1) // 2
+            cut_h = len(halves) // 2
+            for part_f, part_h in ((flips[:cut_f], halves[:cut_h]), (flips[cut_f:], halves[cut_h:])):
+                for src_w, dst_w, eng in part_f:
+                    flip(src_w, dst_w, eng)
+                for n, part in part_h:
+                    multiply_half(n, part)
+                    if part == 1 and n + 1 == EARLY_GROUPS:
+                        done = GRP * EARLY_GROUPS
+                        nc.sync.dma_start(out=out_view[:, :, 0:done], in_=res[:, :, 0:done])
+            if 0 <= w < NG and w + WBUFS < NG:
+                load_w(w + WBUFS)
 
         done = GRP * EARLY_GROUPS
         nc.sync.dma_start(out=out_view[:, :, done:NPOS], in_=res[:, :, done:NPOS])

@@ -5,6 +5,7 @@ from concourse.masks import make_identity
 
 F32 = mybir.dt.float32
 BF16 = mybir.dt.bfloat16
+I32 = mybir.dt.int32
 U32 = mybir.dt.uint32
 U8 = mybir.dt.uint8
 FP8X4 = mybir.dt.float8_e4m3fn_x4
@@ -12,16 +13,18 @@ FP8X4 = mybir.dt.float8_e4m3fn_x4
 P = 128
 B, C, O, ROWS, COLS, KH, KW = 64, 64, 128, 8, 8, 4, 4
 H = 11
-XLEN = C * H * H
+CH = C // 2
+XLEN = CH * H * H
 K = C * KH * KW
+KP = K // 2
 NPOS = ROWS * COLS
 GRP = 4
 NG = NPOS // GRP
-NSUB = 16
+NHR = 2 * ROWS
 WBUFS = 5
 LEAD = 1
-HEAD_SUBS = 3
-XQ = 4
+ROWW = COLS * P
+PAD = B
 EARLY_GROUPS = 12
 FLOPS = 2 * NPOS * B * O * K
 
@@ -29,7 +32,7 @@ FLOPS = 2 * NPOS * B * O * K
 def tile_localconvolution_kernel(tc, x, weight, out):
     nc = tc.nc
     w_view = weight.rearrange("i j o c u v -> o (i j) (c u v)")
-    x_flat = x.rearrange("b c h w -> b (c h w)")
+    x_view = x.rearrange("b (g c) h w -> (b g) (c h w)", g=2)
     out_view = out.rearrange("b o i j -> o b (i j)")
 
     with ExitStack() as ctx:
@@ -37,19 +40,28 @@ def tile_localconvolution_kernel(tc, x, weight, out):
         wraw_pool = ctx.enter_context(tc.tile_pool(name="wraw", bufs=WBUFS))
         gw_pool = ctx.enter_context(tc.tile_pool(name="gw", bufs=3))
         wq_pool = ctx.enter_context(tc.tile_pool(name="wq", bufs=6))
-        pi_pool = ctx.enter_context(tc.tile_pool(name="pi", bufs=HEAD_SUBS))
+        pi_pool = ctx.enter_context(tc.tile_pool(name="pi", bufs=3))
         gp_pool = ctx.enter_context(tc.tile_pool(name="gp", bufs=2))
         tp_pool = ctx.enter_context(tc.psum_pool(name="tp", bufs=6))
         acc_pool = ctx.enter_context(tc.psum_pool(name="acc", bufs=2))
         ctx.enter_context(tc.manual_schedule())
 
+        xs = keep.tile([P, XLEN], BF16, name="xs")
+        nc.sync.dma_start(out=xs[:], in_=x_view)
+        xs_img = xs[:].rearrange("p (c h w) -> p c h w", c=CH, h=H)
+
         ident = keep.tile([P, P], F32, name="ident")
         make_identity(nc, ident[:])
-        xs = keep.tile([P, XLEN], BF16, name="xs")
-        pc = keep.tile([P, 4, COLS, 2, P], U32, name="pc", align_bytes=64)
-        ps = keep.tile([P, 4, COLS, 2, P], U8, name="ps", align_bytes=64)
+        perm = keep.tile([P, P], F32, name="perm")
+        pc = keep.tile([P, ROWS, ROWW + PAD], U32, name="pc", align_bytes=64)
+        ps = keep.tile([P, ROWS, ROWW + PAD], U8, name="ps", align_bytes=64)
         res = keep.tile([P, B, NPOS], F32, name="res")
-        xs_img = xs[:].rearrange("p (c h w) -> p c h w", c=C, h=H)
+        nc.vector.memset(pc[:, :, ROWW:ROWW + PAD].bitcast(I32), 0)
+        nc.vector.memset(ps[:, :, ROWW:ROWW + PAD].bitcast(I32), 0)
+        nc.vector.tensor_copy(
+            out=perm[:].rearrange("p (g b) -> p g b", g=2),
+            in_=ident[:].rearrange("p (b g) -> p g b", g=2),
+        )
 
         wraw = {}
         gw = {}
@@ -57,38 +69,35 @@ def tile_localconvolution_kernel(tc, x, weight, out):
         ws = {}
         pim = {}
         gp = {}
+        accs = {}
 
         def load_w(n):
             t = wraw_pool.tile([P, GRP, K], BF16, name="wraw")
             nc.sync.dma_start(out=t[:], in_=w_view[:, GRP * n:GRP * (n + 1), :])
             wraw[n] = t
 
-        def load_x(cq):
-            lo, hi = XLEN // XQ * cq, XLEN // XQ * (cq + 1)
-            nc.sync.dma_start(out=xs[0:P:2, lo:hi], in_=x_flat[:, lo:hi])
-            hi = min(hi, XLEN - H)
-            nc.sync.dma_start(out=xs[1:P:2, lo:hi], in_=x_flat[:, lo + H:hi + H])
-
-        def flip(src_words, dst_words, engine):
+        def flip(sources, matrix, view, dst_words, engine):
             bank = tp_pool.tile([P, 512], F32, name="tp")
-            for ch in range(4):
-                nc.tensor.transpose(
-                    bank[:, P * ch:P * (ch + 1)],
-                    src_words[:, P * ch:P * (ch + 1)],
-                    ident[:],
-                )
-            view = bank[:].rearrange("p (g m n) -> p g n m", g=2, m=2)
+            for s, src in enumerate(sources):
+                nc.tensor.transpose(bank[:, P * s:P * (s + 1)], src, matrix[:])
             if engine == "s":
-                nc.scalar.copy(out=dst_words, in_=view)
+                nc.scalar.copy(out=dst_words, in_=view(bank))
             else:
-                nc.vector.tensor_copy(out=dst_words, in_=view)
+                nc.vector.tensor_copy(out=dst_words, in_=view(bank))
 
-        def transpose_group(n):
+        def w_view_of(bank):
+            return bank[:].rearrange("p (g m n) -> p g n m", g=2, m=2)
+
+        def p_view_of(bank):
+            return bank[:].rearrange("p (m n) -> p n m", m=2)
+
+        def group_flips(n):
             wf = wraw[n][:].bitcast(F32)
             g_t = gw_pool.tile([P, GRP, 2, O, 4], BF16, name="gw", align_bytes=64)
             gw[n] = g_t
             gf = g_t[:].bitcast(F32)
-            return [(wf[:, a], gf[:, a], "s") for a in range(GRP)]
+            return [([wf[:, a, P * s:P * (s + 1)] for s in range(4)], ident, w_view_of, gf[:, a], "s")
+                    for a in range(GRP)]
 
         def quantise_group(n):
             c_t = wq_pool.tile([P, GRP * 2 * O], U32, name="wc", align_bytes=64)
@@ -101,105 +110,107 @@ def tile_localconvolution_kernel(tc, x, weight, out):
                 in_=gw[n][:].rearrange("p a g o t -> p (a g o t)"),
             )
 
-        def im2col(sub, c0, c1):
-            r, jr = sub // 4, sub % 4
-            if c0 == 0:
-                pim[sub] = pi_pool.tile([P, 2, K], BF16, name="pim")
-            nc.vector.tensor_copy(
-                out=pim[sub][:].rearrange("p q (c u v) -> p c u q v", c=C, u=KH)[:, c0:c1],
-                in_=xs_img[:, c0:c1, 2 * r:2 * r + KH, jr:jr + 2 * KW].rearrange(
-                    "p c u (q v) -> p c u q v", q=2),
-            )
+        def im2col(hr):
+            i = hr // 2
+            t = pi_pool.tile([P, 2, 2, KP], BF16, name="pim")
+            pim[hr] = t
+            for e in range(2):
+                jr = 2 * (hr % 2) + e
+                nc.vector.tensor_copy(
+                    out=t[:, e].rearrange("p q (c u v) -> p c u q v", c=CH, u=KH),
+                    in_=xs_img[:, :, i:i + KH, jr:jr + 2 * KW].rearrange(
+                        "p c u (q v) -> p c u q v", q=2),
+                )
 
-        def transpose_sub(sub):
-            half = sub // 2
-            if sub % 2 == 0:
-                gp[half] = gp_pool.tile([P, 4, 2, P, 4], BF16, name="gp", align_bytes=64)
-            gf = gp[half][:].bitcast(F32)
-            pf = pim[sub][:].bitcast(F32)
-            return [(pf[:, q], gf[:, 2 * (sub % 2) + q], "s" if q == 0 else "v") for q in range(2)]
+        def half_row_flips(hr):
+            i = hr // 2
+            if hr % 2 == 0:
+                gp[i] = gp_pool.tile([P, COLS, 2, B, 4], BF16, name="gp", align_bytes=64)
+            gf = gp[i][:].bitcast(F32)
+            pf = pim[hr][:].bitcast(F32)
+            flips = []
+            for e in range(2):
+                jr = 2 * (hr % 2) + e
+                flips.append((
+                    [pf[:, e, q, P * m:P * (m + 1)] for m in range(2) for q in range(2)],
+                    perm, p_view_of,
+                    gf[:, 2 * jr:2 * jr + 2].rearrange("p a g b m -> p (a g b) m"),
+                    "s" if e == 0 else "v",
+                ))
+            return flips
 
-        def quantise_half(half):
-            r, hh = half // 2, half % 2
+        def quantise_row(i):
             nc.vector.quantize_mx(
-                out=pc[:, r, 4 * hh:4 * hh + 4].rearrange("p a g n -> p (a g n)").bitcast(FP8X4),
-                scales=ps[:, r, 4 * hh:4 * hh + 4].rearrange("p a g n -> p (a g n)"),
-                in_=gp[half][:].rearrange("p a g n t -> p (a g n t)"),
+                out=pc[:, i, 0:ROWW].bitcast(FP8X4),
+                scales=ps[:, i, 0:ROWW],
+                in_=gp[i][:].rearrange("p a g b t -> p (a g b t)"),
             )
-
-        accs = {}
 
         def multiply_half(n, part):
             i, jh = n // 2, n % 2
-            r, s = i // 2, i % 2
             if part == 0:
                 accs[n] = acc_pool.tile([P, 512], F32, name="acc")
             acc = accs[n]
             for a in range(2 * part, 2 * part + 2):
                 for g in range(2):
                     lo = (2 * a + g) * O
+                    col = P * (2 * a + jh) + B * g
                     nc.tensor.matmul_mx(
                         out=acc[:, P * a:P * (a + 1)],
                         lhsT=wc[n][:, lo:lo + O].bitcast(FP8X4),
                         lhsT_scale=ws[n][:, lo:lo + O],
-                        rhs=pc[:, r, 2 * a + jh, g, :].bitcast(FP8X4),
-                        rhs_scale=ps[:, r, 2 * a + jh, g, :],
+                        rhs=pc[:, i, col:col + P].bitcast(FP8X4),
+                        rhs_scale=ps[:, i, col:col + P],
                         start=(g == 0),
                         stop=(g == 1),
                     )
             if part == 1:
                 nc.scalar.copy(
                     out=res[:, :, GRP * n:GRP * (n + 1)],
-                    in_=acc[:].rearrange("p (a b s) -> p s b a", a=GRP, s=2)[:, s],
+                    in_=acc[:].rearrange("p (a h b) -> p h b a", a=GRP, h=2)[:, 0],
                 )
 
-        for cq in range(XQ):
-            load_x(cq)
         for n in range(WBUFS):
             load_w(n)
-        cw = C // XQ
-        for cq in range(XQ):
-            for sub in range(HEAD_SUBS):
-                im2col(sub, cw * cq, cw * (cq + 1))
+        im2col(0)
 
         next_m = 0
-        half_step = {}
-        pending_half = []
+        row_step = {}
+        pending_rows = []
+        done = GRP * EARLY_GROUPS
         for t in range(NG + LEAD + 3):
             w = t - LEAD
             if 1 <= w <= NG:
                 quantise_group(w - 1)
-            for half in pending_half:
-                quantise_half(half)
-                half_step[half] = t
-            pending_half = []
-            if HEAD_SUBS <= t + 1 < NSUB:
-                im2col(t + 1, 0, C)
+            for i in pending_rows:
+                quantise_row(i)
+                row_step[i] = t
+            pending_rows = []
+            if t + 1 < NHR:
+                im2col(t + 1)
             flips = []
             if 0 <= w < NG:
-                flips.extend(transpose_group(w))
-            if t < NSUB:
-                flips.extend(transpose_sub(t))
+                flips.extend(group_flips(w))
+            if t < NHR:
+                flips.extend(half_row_flips(t))
                 if t % 2 == 1:
-                    pending_half.append(t // 2)
+                    pending_rows.append(t // 2)
             halves = []
             while next_m < NG and next_m <= w - 2 and len(halves) < 4:
-                if half_step.get(2 * (next_m // 4) + 1, t) >= t:
+                if row_step.get(next_m // 2, t) >= t:
                     break
                 halves.extend([(next_m, 0), (next_m, 1)])
                 next_m += 1
             cut_f = (len(flips) + 1) // 2
             cut_h = len(halves) // 2
             for part_f, part_h in ((flips[:cut_f], halves[:cut_h]), (flips[cut_f:], halves[cut_h:])):
-                for src_w, dst_w, eng in part_f:
-                    flip(src_w, dst_w, eng)
+                for sources, matrix, view, dst_w, eng in part_f:
+                    flip(sources, matrix, view, dst_w, eng)
                 for n, part in part_h:
                     multiply_half(n, part)
                     if part == 1 and n + 1 == EARLY_GROUPS:
-                        done = GRP * EARLY_GROUPS
                         nc.sync.dma_start(out=out_view[:, :, 0:done], in_=res[:, :, 0:done])
             if 0 <= w < NG and w + WBUFS < NG:
                 load_w(w + WBUFS)
 
-        done = GRP * EARLY_GROUPS
         nc.sync.dma_start(out=out_view[:, :, done:NPOS], in_=res[:, :, done:NPOS])

@@ -26,6 +26,7 @@ LEAD = 1
 ROWW = COLS * P
 PAD = B
 EARLY_GROUPS = 12
+WARM_PASSES = 12
 FLOPS = 2 * NPOS * B * O * K
 
 
@@ -56,6 +57,11 @@ def tile_localconvolution_kernel(tc, x, weight, out):
         pc = keep.tile([P, ROWS, ROWW + PAD], U32, name="pc", align_bytes=64)
         ps = keep.tile([P, ROWS, ROWW + PAD], U8, name="ps", align_bytes=64)
         res = keep.tile([P, B, NPOS], F32, name="res")
+        zc = keep.tile([P, 512], U32, name="zc", align_bytes=64)
+        zs = keep.tile([P, 512], U8, name="zs", align_bytes=64)
+        zb = keep.tile([P, 2048], BF16, name="zb", align_bytes=64)
+        nc.vector.memset(zb[:].bitcast(I32), 0)
+        nc.vector.quantize_mx(out=zc[:].bitcast(FP8X4), scales=zs[:], in_=zb[:])
         nc.vector.memset(pc[:, :, ROWW:ROWW + PAD].bitcast(I32), 0)
         nc.vector.memset(ps[:, :, ROWW:ROWW + PAD].bitcast(I32), 0)
         nc.vector.tensor_copy(
@@ -170,9 +176,24 @@ def tile_localconvolution_kernel(tc, x, weight, out):
                     in_=acc[:].rearrange("p (a h b) -> p h b a", a=GRP, h=2)[:, 0],
                 )
 
+        warm = acc_pool.tile([P, 512], F32, name="acc")
+
+        def idle_pass():
+            nc.tensor.matmul_mx(
+                out=warm[:],
+                lhsT=zc[:, 0:P].bitcast(FP8X4),
+                lhsT_scale=zs[:, 0:P],
+                rhs=zc[:].bitcast(FP8X4),
+                rhs_scale=zs[:],
+                start=True,
+                stop=True,
+            )
+
         for n in range(WBUFS):
             load_w(n)
         im2col(0)
+        for n in range(WARM_PASSES):
+            idle_pass()
 
         next_m = 0
         row_step = {}
@@ -189,12 +210,14 @@ def tile_localconvolution_kernel(tc, x, weight, out):
             if t + 1 < NHR:
                 im2col(t + 1)
             flips = []
-            if 0 <= w < NG:
+            if 1 <= w < NG:
                 flips.extend(group_flips(w))
             if t < NHR:
                 flips.extend(half_row_flips(t))
                 if t % 2 == 1:
                     pending_rows.append(t // 2)
+            if w == 0:
+                flips.extend(group_flips(w))
             halves = []
             while next_m < NG and next_m <= w - 2 and len(halves) < 4:
                 if row_step.get(next_m // 2, t) >= t:
@@ -206,6 +229,8 @@ def tile_localconvolution_kernel(tc, x, weight, out):
             for part_f, part_h in ((flips[:cut_f], halves[:cut_h]), (flips[cut_f:], halves[cut_h:])):
                 for sources, matrix, view, dst_w, eng in part_f:
                     flip(sources, matrix, view, dst_w, eng)
+                if w < 2:
+                    idle_pass()
                 for n, part in part_h:
                     multiply_half(n, part)
                     if part == 1 and n + 1 == EARLY_GROUPS:

@@ -26,7 +26,6 @@ LEAD = 1
 ROWW = COLS * P
 PAD = B
 EARLY_GROUPS = 12
-WARM_PASSES = 12
 FLOPS = 2 * NPOS * B * O * K
 
 
@@ -45,7 +44,6 @@ def tile_localconvolution_kernel(tc, x, weight, out):
         gp_pool = ctx.enter_context(tc.tile_pool(name="gp", bufs=2))
         tp_pool = ctx.enter_context(tc.psum_pool(name="tp", bufs=6))
         acc_pool = ctx.enter_context(tc.psum_pool(name="acc", bufs=2))
-        ctx.enter_context(tc.manual_schedule())
 
         xs = keep.tile([P, XLEN], BF16, name="xs")
         nc.sync.dma_start(out=xs[:], in_=x_view)
@@ -57,11 +55,6 @@ def tile_localconvolution_kernel(tc, x, weight, out):
         pc = keep.tile([P, ROWS, ROWW + PAD], U32, name="pc", align_bytes=64)
         ps = keep.tile([P, ROWS, ROWW + PAD], U8, name="ps", align_bytes=64)
         res = keep.tile([P, B, NPOS], F32, name="res")
-        zc = keep.tile([P, 512], U32, name="zc", align_bytes=64)
-        zs = keep.tile([P, 512], U8, name="zs", align_bytes=64)
-        zb = keep.tile([P, 2048], BF16, name="zb", align_bytes=64)
-        nc.vector.memset(zb[:].bitcast(I32), 0)
-        nc.vector.quantize_mx(out=zc[:].bitcast(FP8X4), scales=zs[:], in_=zb[:])
         nc.vector.memset(pc[:, :, ROWW:ROWW + PAD].bitcast(I32), 0)
         nc.vector.memset(ps[:, :, ROWW:ROWW + PAD].bitcast(I32), 0)
         nc.vector.tensor_copy(
@@ -176,24 +169,9 @@ def tile_localconvolution_kernel(tc, x, weight, out):
                     in_=acc[:].rearrange("p (a h b) -> p h b a", a=GRP, h=2)[:, 0],
                 )
 
-        warm = acc_pool.tile([P, 512], F32, name="acc")
-
-        def idle_pass():
-            nc.tensor.matmul_mx(
-                out=warm[:],
-                lhsT=zc[:, 0:P].bitcast(FP8X4),
-                lhsT_scale=zs[:, 0:P],
-                rhs=zc[:].bitcast(FP8X4),
-                rhs_scale=zs[:],
-                start=True,
-                stop=True,
-            )
-
         for n in range(WBUFS):
             load_w(n)
         im2col(0)
-        for n in range(WARM_PASSES):
-            idle_pass()
 
         next_m = 0
         row_step = {}
@@ -210,14 +188,12 @@ def tile_localconvolution_kernel(tc, x, weight, out):
             if t + 1 < NHR:
                 im2col(t + 1)
             flips = []
-            if 1 <= w < NG:
+            if 0 <= w < NG:
                 flips.extend(group_flips(w))
             if t < NHR:
                 flips.extend(half_row_flips(t))
                 if t % 2 == 1:
                     pending_rows.append(t // 2)
-            if w == 0:
-                flips.extend(group_flips(w))
             halves = []
             while next_m < NG and next_m <= w - 2 and len(halves) < 4:
                 if row_step.get(next_m // 2, t) >= t:
@@ -229,8 +205,6 @@ def tile_localconvolution_kernel(tc, x, weight, out):
             for part_f, part_h in ((flips[:cut_f], halves[:cut_h]), (flips[cut_f:], halves[cut_h:])):
                 for sources, matrix, view, dst_w, eng in part_f:
                     flip(sources, matrix, view, dst_w, eng)
-                if w < 2:
-                    idle_pass()
                 for n, part in part_h:
                     multiply_half(n, part)
                     if part == 1 and n + 1 == EARLY_GROUPS:

@@ -44,6 +44,7 @@ def tile_localconvolution_kernel(tc, x, weight, out):
         gp_pool = ctx.enter_context(tc.tile_pool(name="gp", bufs=2))
         tp_pool = ctx.enter_context(tc.psum_pool(name="tp", bufs=6))
         acc_pool = ctx.enter_context(tc.psum_pool(name="acc", bufs=2))
+        ctx.enter_context(tc.manual_schedule())
 
         xs = keep.tile([P, XLEN], BF16, name="xs")
         nc.sync.dma_start(out=xs[:], in_=x_view)
@@ -145,12 +146,13 @@ def tile_localconvolution_kernel(tc, x, weight, out):
                 in_=gp[i][:].rearrange("p a g b t -> p (a g b t)"),
             )
 
-        def multiply_half(n, part):
+        def multiply_position(pos):
+            n, a = pos // GRP, pos % GRP
             i, jh = n // 2, n % 2
-            if part == 0:
+            if a == 0:
                 accs[n] = acc_pool.tile([P, 512], F32, name="acc")
             acc = accs[n]
-            for a in range(2 * part, 2 * part + 2):
+            for a in range(a, a + 1):
                 for g in range(2):
                     lo = (2 * a + g) * O
                     col = P * (2 * a + jh) + B * g
@@ -163,17 +165,20 @@ def tile_localconvolution_kernel(tc, x, weight, out):
                         start=(g == 0),
                         stop=(g == 1),
                     )
-            if part == 1:
+            if pos % GRP == GRP - 1:
                 nc.scalar.copy(
                     out=res[:, :, GRP * n:GRP * (n + 1)],
                     in_=acc[:].rearrange("p (a h b) -> p h b a", a=GRP, h=2)[:, 0],
                 )
+                if n + 1 == EARLY_GROUPS:
+                    nc.sync.dma_start(out=out_view[:, :, 0:done], in_=res[:, :, 0:done])
 
         for n in range(WBUFS):
             load_w(n)
         im2col(0)
 
-        next_m = 0
+        banks_done = 0
+        pos_done = 0
         row_step = {}
         pending_rows = []
         done = GRP * EARLY_GROUPS
@@ -194,21 +199,17 @@ def tile_localconvolution_kernel(tc, x, weight, out):
                 flips.extend(half_row_flips(t))
                 if t % 2 == 1:
                     pending_rows.append(t // 2)
-            halves = []
-            while next_m < NG and next_m <= w - 2 and len(halves) < 4:
-                if row_step.get(next_m // 2, t) >= t:
-                    break
-                halves.extend([(next_m, 0), (next_m, 1)])
-                next_m += 1
-            cut_f = (len(flips) + 1) // 2
-            cut_h = len(halves) // 2
-            for part_f, part_h in ((flips[:cut_f], halves[:cut_h]), (flips[cut_f:], halves[cut_h:])):
-                for sources, matrix, view, dst_w, eng in part_f:
-                    flip(sources, matrix, view, dst_w, eng)
-                for n, part in part_h:
-                    multiply_half(n, part)
-                    if part == 1 and n + 1 == EARLY_GROUPS:
-                        nc.sync.dma_start(out=out_view[:, :, 0:done], in_=res[:, :, 0:done])
+            for sources, matrix, view, dst_w, eng in flips:
+                flip(sources, matrix, view, dst_w, eng)
+                banks_done += 1
+                if banks_done % 4 == 0:
+                    while pos_done < (2 * banks_done - 28) // 3:
+                        multiply_position(pos_done)
+                        pos_done += 1
+            if w >= NG - 1:
+                while pos_done < min(NPOS, GRP * (t - 2)):
+                    multiply_position(pos_done)
+                    pos_done += 1
             if 0 <= w < NG and w + WBUFS < NG:
                 load_w(w + WBUFS)
 

from contextlib import ExitStack

import concourse.mybir as mybir
from concourse.masks import make_identity

F32 = mybir.dt.float32
BF16 = mybir.dt.bfloat16
I32 = mybir.dt.int32
U32 = mybir.dt.uint32
U8 = mybir.dt.uint8
FP8X4 = mybir.dt.float8_e4m3fn_x4

P = 128
B, C, O, ROWS, COLS, KH, KW = 64, 64, 128, 8, 8, 4, 4
H = 11
CH = C // 2
XLEN = CH * H * H
K = C * KH * KW
KP = K // 2
NPOS = ROWS * COLS
GRP = 4
NG = NPOS // GRP
NHR = 2 * ROWS
WBUFS = 5
LEAD = 1
ROWW = COLS * P
PAD = B
EARLY_GROUPS = 12
FLOPS = 2 * NPOS * B * O * K


def tile_localconvolution_kernel(tc, x, weight, out):
    nc = tc.nc
    w_view = weight.rearrange("i j o c u v -> o (i j) (c u v)")
    x_view = x.rearrange("b (g c) h w -> (b g) (c h w)", g=2)
    out_view = out.rearrange("b o i j -> o b (i j)")

    with ExitStack() as ctx:
        keep = ctx.enter_context(tc.tile_pool(name="keep", bufs=1))
        wraw_pool = ctx.enter_context(tc.tile_pool(name="wraw", bufs=WBUFS))
        gw_pool = ctx.enter_context(tc.tile_pool(name="gw", bufs=3))
        wq_pool = ctx.enter_context(tc.tile_pool(name="wq", bufs=6))
        pi_pool = ctx.enter_context(tc.tile_pool(name="pi", bufs=3))
        gp_pool = ctx.enter_context(tc.tile_pool(name="gp", bufs=2))
        tp_pool = ctx.enter_context(tc.psum_pool(name="tp", bufs=6))
        acc_pool = ctx.enter_context(tc.psum_pool(name="acc", bufs=2))
        ctx.enter_context(tc.manual_schedule())

        xs = keep.tile([P, XLEN], BF16, name="xs")
        nc.sync.dma_start(out=xs[:], in_=x_view)
        xs_img = xs[:].rearrange("p (c h w) -> p c h w", c=CH, h=H)

        ident = keep.tile([P, P], F32, name="ident")
        make_identity(nc, ident[:])
        perm = keep.tile([P, P], F32, name="perm")
        pc = keep.tile([P, ROWS, ROWW + PAD], U32, name="pc", align_bytes=64)
        ps = keep.tile([P, ROWS, ROWW + PAD], U8, name="ps", align_bytes=64)
        res = keep.tile([P, B, NPOS], F32, name="res")
        nc.vector.memset(pc[:, :, ROWW:ROWW + PAD].bitcast(I32), 0)
        nc.vector.memset(ps[:, :, ROWW:ROWW + PAD].bitcast(I32), 0)
        nc.vector.tensor_copy(
            out=perm[:].rearrange("p (g b) -> p g b", g=2),
            in_=ident[:].rearrange("p (b g) -> p g b", g=2),
        )

        wraw = {}
        gw = {}
        wc = {}
        ws = {}
        pim = {}
        gp = {}
        accs = {}

        def load_w(n):
            t = wraw_pool.tile([P, GRP, K], BF16, name="wraw")
            nc.sync.dma_start(out=t[:], in_=w_view[:, GRP * n:GRP * (n + 1), :])
            wraw[n] = t

        def flip(sources, matrix, view, dst_words, engine):
            bank = tp_pool.tile([P, 512], F32, name="tp")
            for s, src in enumerate(sources):
                nc.tensor.transpose(bank[:, P * s:P * (s + 1)], src, matrix[:])
            if engine == "s":
                nc.scalar.copy(out=dst_words, in_=view(bank))
            else:
                nc.vector.tensor_copy(out=dst_words, in_=view(bank))

        def w_view_of(bank):
            return bank[:].rearrange("p (g m n) -> p g n m", g=2, m=2)

        def p_view_of(bank):
            return bank[:].rearrange("p (m n) -> p n m", m=2)

        def group_flips(n):
            wf = wraw[n][:].bitcast(F32)
            g_t = gw_pool.tile([P, GRP, 2, O, 4], BF16, name="gw", align_bytes=64)
            gw[n] = g_t
            gf = g_t[:].bitcast(F32)
            return [([wf[:, a, P * s:P * (s + 1)] for s in range(4)], ident, w_view_of, gf[:, a], "s")
                    for a in range(GRP)]

        def quantise_group(n):
            c_t = wq_pool.tile([P, GRP * 2 * O], U32, name="wc", align_bytes=64)
            s_t = wq_pool.tile([P, GRP * 2 * O], U8, name="ws", align_bytes=64)
            wc[n] = c_t
            ws[n] = s_t
            nc.vector.quantize_mx(
                out=c_t[:].bitcast(FP8X4),
                scales=s_t[:],
                in_=gw[n][:].rearrange("p a g o t -> p (a g o t)"),
            )

        def im2col(hr):
            i = hr // 2
            t = pi_pool.tile([P, 2, 2, KP], BF16, name="pim")
            pim[hr] = t
            for e in range(2):
                jr = 2 * (hr % 2) + e
                nc.vector.tensor_copy(
                    out=t[:, e].rearrange("p q (c u v) -> p c u q v", c=CH, u=KH),
                    in_=xs_img[:, :, i:i + KH, jr:jr + 2 * KW].rearrange(
                        "p c u (q v) -> p c u q v", q=2),
                )

        def half_row_flips(hr):
            i = hr // 2
            if hr % 2 == 0:
                gp[i] = gp_pool.tile([P, COLS, 2, B, 4], BF16, name="gp", align_bytes=64)
            gf = gp[i][:].bitcast(F32)
            pf = pim[hr][:].bitcast(F32)
            flips = []
            for e in range(2):
                jr = 2 * (hr % 2) + e
                flips.append((
                    [pf[:, e, q, P * m:P * (m + 1)] for m in range(2) for q in range(2)],
                    perm, p_view_of,
                    gf[:, 2 * jr:2 * jr + 2].rearrange("p a g b m -> p (a g b) m"),
                    "s" if e == 0 else "v",
                ))
            return flips

        def quantise_row(i):
            nc.vector.quantize_mx(
                out=pc[:, i, 0:ROWW].bitcast(FP8X4),
                scales=ps[:, i, 0:ROWW],
                in_=gp[i][:].rearrange("p a g b t -> p (a g b t)"),
            )

        def multiply_position(pos):
            n, a = pos // GRP, pos % GRP
            i, jh = n // 2, n % 2
            if a == 0:
                accs[n] = acc_pool.tile([P, 512], F32, name="acc")
            acc = accs[n]
            for a in range(a, a + 1):
                for g in range(2):
                    lo = (2 * a + g) * O
                    col = P * (2 * a + jh) + B * g
                    nc.tensor.matmul_mx(
                        out=acc[:, P * a:P * (a + 1)],
                        lhsT=wc[n][:, lo:lo + O].bitcast(FP8X4),
                        lhsT_scale=ws[n][:, lo:lo + O],
                        rhs=pc[:, i, col:col + P].bitcast(FP8X4),
                        rhs_scale=ps[:, i, col:col + P],
                        start=(g == 0),
                        stop=(g == 1),
                    )
            if pos % GRP == GRP - 1:
                nc.scalar.copy(
                    out=res[:, :, GRP * n:GRP * (n + 1)],
                    in_=acc[:].rearrange("p (a h b) -> p h b a", a=GRP, h=2)[:, 0],
                )
                if n + 1 == EARLY_GROUPS:
                    nc.sync.dma_start(out=out_view[:, :, 0:done], in_=res[:, :, 0:done])

        for n in range(WBUFS):
            load_w(n)
        im2col(0)

        banks_done = 0
        pos_done = 0
        row_step = {}
        pending_rows = []
        done = GRP * EARLY_GROUPS
        for t in range(NG + LEAD + 3):
            w = t - LEAD
            if 1 <= w <= NG:
                quantise_group(w - 1)
            for i in pending_rows:
                quantise_row(i)
                row_step[i] = t
            pending_rows = []
            if t + 1 < NHR:
                im2col(t + 1)
            flips = []
            if 0 <= w < NG:
                flips.extend(group_flips(w))
            if t < NHR:
                flips.extend(half_row_flips(t))
                if t % 2 == 1:
                    pending_rows.append(t // 2)
            for sources, matrix, view, dst_w, eng in flips:
                flip(sources, matrix, view, dst_w, eng)
                banks_done += 1
                if banks_done % 4 == 0:
                    while pos_done < (2 * banks_done - 28) // 3:
                        multiply_position(pos_done)
                        pos_done += 1
            if w >= NG - 1:
                while pos_done < min(NPOS, GRP * (t - 2)):
                    multiply_position(pos_done)
                    pos_done += 1
            if 0 <= w < NG and w + WBUFS < NG:
                load_w(w + WBUFS)

        nc.sync.dma_start(out=out_view[:, :, done:NPOS], in_=res[:, :, done:NPOS])
